import numpy as np
import ml_dtypes


def mxq(x, axis, fmt="e4m3"):
    dtype, down = {"e4m3": (ml_dtypes.float8_e4m3fn, 7), "e5m2": (ml_dtypes.float8_e5m2, 14)}[fmt]
    v = np.moveaxis(np.asarray(x, np.float32).astype(ml_dtypes.bfloat16).astype(np.float64), axis, -1)
    blocks = v.reshape(v.shape[:-1] + (-1, 32))
    amax = np.abs(blocks).max(-1, keepdims=True)
    byte = np.maximum(np.where(amax > 0, np.frexp(amax)[1] - 1 + 127, 0) - down, 1)
    scale = np.exp2(byte - 127.0)
    codes = (blocks / scale).astype(np.float32).astype(dtype).astype(np.float64)
    return np.moveaxis((codes * scale).reshape(v.shape), -1, axis)


WIDE = False


def mx_kscale(k):
    if not WIDE:
        return np.ones(k)
    levels = np.array([10, -10, 5, -5, 0])
    a = np.random.permutation(np.resize(levels, k // 512 * 4)).reshape(k // 512, 4)
    idx = np.arange(k)
    return np.exp2(a[idx // 512, idx % 128 // 32])


BF16 = ml_dtypes.bfloat16


def bf(x):
    return np.asarray(x, np.float32).astype(BF16)


def f64(x):
    return np.asarray(x).astype(np.float64)


B, S, D, H, HD = 4, 128, 2048, 16, 128
E = H * HD
HALF = HD // 2


def rope(t, fc, fs):
    p = t.reshape(B, S, H, HALF, 2)
    tr, ti = p[..., 0], p[..., 1]
    return np.stack([tr * fc - ti * fs, tr * fs + ti * fc], axis=-1).reshape(B, S, H, HD)


def setup_inputs():
    s = mx_kscale(D)
    return {"x": bf(np.random.standard_normal((B, S, D)) * s),
            "freq_cos": bf(np.cos(np.random.standard_normal((S, HALF)))),
            "freq_sin": bf(np.sin(np.random.standard_normal((S, HALF)))),
            "wq": bf(np.random.standard_normal((E, D)) / np.sqrt(D) / s[None, :]),
            "wk": bf(np.random.standard_normal((E, D)) / np.sqrt(D) / s[None, :])}


def reference(x, freq_cos, freq_sin, wq, wk):
    xq = mxq(f64(x), 2, "e4m3")
    q = (xq @ mxq(f64(wq), 1, "e4m3").T).reshape(B, S, H, HD)
    k = (xq @ mxq(f64(wk), 1, "e4m3").T).reshape(B, S, H, HD)
    fc = f64(freq_cos)[None, :, None, :]
    fs = f64(freq_sin)[None, :, None, :]
    q_rot = rope(q, fc, fs).transpose(0, 2, 1, 3)
    k_rot = rope(k, fc, fs).transpose(0, 2, 1, 3)
    return q_rot, k_rot

@@ -1,0 +1,177 @@
+from contextlib import ExitStack
+
+import concourse.mybir as mybir
+from concourse.masks import make_identity
+
+F32 = mybir.dt.float32
+BF16 = mybir.dt.bfloat16
+U32 = mybir.dt.uint32
+U8 = mybir.dt.uint8
+FP8X4 = mybir.dt.float8_e4m3fn_x4
+MULT = mybir.AluOpType.mult
+ADD = mybir.AluOpType.add
+
+B, S, D, H, HD = 4, 128, 2048, 16, 128
+HALF = HD // 2
+P = 128
+K_PASS = 4 * P
+PASSES = D // K_PASS
+WORDS = D // 2
+SLAB = 2 * P
+SLAB_HEADS = SLAB // HD
+X_SLABS = B * S // SLAB
+W_SLABS = H * HD // SLAB
+BANK = 512
+RAW_BUFS = 12
+
+FLOPS = 2 * (B * S) * D * (2 * H * HD)
+
+
+def tile_attention_pa_kernel(tc, x, freq_cos, freq_sin, wq, wk, out_0, out_1):
+    nc = tc.nc
+
+    slabs = [x[2 * n : 2 * n + 2].rearrange("b s k -> s b k") for n in range(X_SLABS)]
+    for w in (wq, wk):
+        for n in range(W_SLABS):
+            slabs.append(w[n * SLAB : (n + 1) * SLAB, :].rearrange("(c i) k -> c i k", i=2))
+    targets = [(out, n * SLAB_HEADS) for out in (out_0, out_1) for n in range(W_SLABS)]
+
+    with ExitStack() as ctx:
+        keep = ctx.enter_context(tc.tile_pool(name="keep", bufs=1))
+        raw_pool = ctx.enter_context(tc.tile_pool(name="raw", bufs=RAW_BUFS))
+        grouped_pool = ctx.enter_context(tc.tile_pool(name="grouped", bufs=3))
+        w_pool = ctx.enter_context(tc.tile_pool(name="w_mx", bufs=3))
+        rope_pool = ctx.enter_context(tc.tile_pool(name="rope", bufs=3))
+        result_pool = ctx.enter_context(tc.tile_pool(name="result", bufs=6))
+        turned_pool = ctx.enter_context(tc.psum_pool(name="turned", bufs=4))
+        product_pool = ctx.enter_context(tc.psum_pool(name="product", bufs=4))
+        ctx.enter_context(tc.manual_schedule())
+
+        raw_tiles = {}
+        grouped_tiles = {}
+        mx_tiles = {}
+
+        def load(n):
+            raw = raw_pool.tile([P, 2 * D], BF16)
+            nc.sync.dma_start(out=raw[:].rearrange("p (r k) -> p r k", r=2), in_=slabs[n])
+            raw_tiles[n] = raw
+
+        def transpose_and_regroup(n):
+            words = raw_tiles[n][:].bitcast(F32)
+            grouped = grouped_pool.tile([P, PASSES * SLAB * 4], BF16, align_bytes=64)
+            grouped_words = grouped[:].bitcast(F32).rearrange(
+                "p (g r c u) -> p g r c u", g=PASSES, r=2, u=2
+            )
+            for g in range(PASSES):
+                turned = turned_pool.tile([P, 2, 2, P], F32)
+                for r in range(2):
+                    for u in range(2):
+                        first = r * WORDS + (2 * g + u) * P
+                        nc.tensor.transpose(turned[:, r, u, :], words[:, first : first + P], ident[:])
+                nc.scalar.copy(out=grouped_words[:, g], in_=turned[:].rearrange("p r u c -> p r c u"))
+            grouped_tiles[n] = grouped
+
+        def new_mx_tiles(n):
+            pool, label = (keep, "x%d" % n) if n < X_SLABS else (w_pool, "w")
+            codes = pool.tile([P, PASSES * SLAB], U32, name=label + "_codes", align_bytes=64)
+            scales = pool.tile([P, PASSES * SLAB], U8, name=label + "_scales", align_bytes=64)
+            mx_tiles[n] = (codes, scales)
+
+        def quantise(n, half):
+            codes, scales = mx_tiles[n]
+            cols = slice(half * 2 * SLAB, (half + 1) * 2 * SLAB)
+            nc.vector.quantize_mx(
+                out=codes[:, cols].bitcast(FP8X4),
+                scales=scales[:, cols],
+                in_=grouped_tiles[n][:, half * 8 * SLAB : (half + 1) * 8 * SLAB],
+            )
+
+        def multiply(n, x_slab):
+            x_codes, x_scales = mx_tiles[x_slab]
+            w_codes, w_scales = mx_tiles[n]
+            product = product_pool.tile([P, BANK], F32)
+            for entry in range(2):
+                for g in range(PASSES):
+                    x_cols = slice(g * SLAB + entry * P, g * SLAB + (entry + 1) * P)
+                    w_cols = slice(g * SLAB, (g + 1) * SLAB)
+                    nc.tensor.matmul_mx(
+                        out=product[:, entry * SLAB : (entry + 1) * SLAB],
+                        lhsT=x_codes[:, x_cols].bitcast(FP8X4),
+                        lhsT_scale=x_scales[:, x_cols],
+                        rhs=w_codes[:, w_cols].bitcast(FP8X4),
+                        rhs_scale=w_scales[:, w_cols],
+                        start=(g == 0),
+                        stop=(g == PASSES - 1),
+                    )
+            return product
+
+        def rotate_and_store(product, x_slab, target):
+            planes = product[:].rearrange("p (b i c) -> p b i c", b=2, i=2)
+            twice = [P, 2, P, 2]
+            from_even = rope_pool.tile([P, BANK], F32)
+            nc.vector.tensor_tensor(
+                out=from_even[:].rearrange("p (b c i) -> p b c i", b=2, i=2),
+                in0=planes[:, :, 0, :].unsqueeze(3).to_broadcast(twice),
+                in1=cos_sin[:].rearrange("p (b c i) -> p b c i", b=2, i=2),
+                op=MULT,
+            )
+            from_odd = rope_pool.tile([P, BANK], F32)
+            nc.vector.tensor_tensor(
+                out=from_odd[:].rearrange("p (b c i) -> p b c i", b=2, i=2),
+                in0=planes[:, :, 1, :].unsqueeze(3).to_broadcast(twice),
+                in1=minus_sin_cos[:].rearrange("p (b c i) -> p b c i", b=2, i=2),
+                op=MULT,
+            )
+            rotated = result_pool.tile([P, BANK], F32)
+            nc.gpsimd.tensor_tensor(out=rotated[:], in0=from_even[:], in1=from_odd[:], op=ADD)
+            out, first_head = target
+            for entry in range(2):
+                nc.sync.dma_start(
+                    out=out[2 * x_slab + entry, first_head : first_head + SLAB_HEADS].rearrange(
+                        "h s d -> s h d"
+                    ),
+                    in_=rotated[:, entry * SLAB : (entry + 1) * SLAB].rearrange(
+                        "p (h d) -> p h d", h=SLAB_HEADS
+                    ),
+                )
+
+        cos_bf = keep.tile([P, HALF], BF16)
+        sin_bf = keep.tile([P, HALF], BF16)
+        nc.scalar.dma_start(out=cos_bf[:], in_=freq_cos)
+        nc.scalar.dma_start(out=sin_bf[:], in_=freq_sin)
+        for n in range(RAW_BUFS):
+            load(n)
+
+        ident = keep.tile([P, P], F32)
+        make_identity(nc, ident[:])
+
+        repeats = BANK // HD
+        cos_sin = keep.tile([P, BANK], F32)
+        minus_sin_cos = keep.tile([P, BANK], F32)
+        cos_sin_view = cos_sin[:].rearrange("p (n j i) -> p n j i", n=repeats, i=2)
+        minus_sin_cos_view = minus_sin_cos[:].rearrange("p (n j i) -> p n j i", n=repeats, i=2)
+        cos_repeated = cos_bf[:].unsqueeze(1).to_broadcast([P, repeats, HALF])
+        sin_repeated = sin_bf[:].unsqueeze(1).to_broadcast([P, repeats, HALF])
+        nc.vector.tensor_copy(out=cos_sin_view[:, :, :, 0], in_=cos_repeated)
+        nc.vector.tensor_copy(out=cos_sin_view[:, :, :, 1], in_=sin_repeated)
+        nc.vector.tensor_scalar_mul(out=minus_sin_cos_view[:, :, :, 0], in0=sin_repeated, scalar1=-1.0)
+        nc.vector.tensor_copy(out=minus_sin_cos_view[:, :, :, 1], in_=cos_repeated)
+
+        for n in range(X_SLABS + 1):
+            transpose_and_regroup(n)
+            new_mx_tiles(n)
+            quantise(n, 0)
+            quantise(n, 1)
+
+        last = len(slabs) - 1
+        for n in range(X_SLABS, len(slabs)):
+            if n - X_SLABS + RAW_BUFS <= last:
+                load(n - X_SLABS + RAW_BUFS)
+            if n < last:
+                transpose_and_regroup(n + 1)
+                new_mx_tiles(n + 1)
+            products = [multiply(n, x_slab) for x_slab in range(X_SLABS)]
+            for part in range(2):
+                if n < last:
+                    quantise(n + 1, part)
+                rotate_and_store(products[part], part, targets[n - X_SLABS])

@@ -23,6 +23,7 @@ X_SLABS = B * S // SLAB
 W_SLABS = H * HD // SLAB
 BANK = 512
 RAW_BUFS = 12
+AHEAD = 2
 
 FLOPS = 2 * (B * S) * D * (2 * H * HD)
 
@@ -40,9 +41,9 @@ def tile_attention_pa_kernel(tc, x, freq_cos, freq_sin, wq, wk, out_0, out_1):
         keep = ctx.enter_context(tc.tile_pool(name="keep", bufs=1))
         raw_pool = ctx.enter_context(tc.tile_pool(name="raw", bufs=RAW_BUFS))
         grouped_pool = ctx.enter_context(tc.tile_pool(name="grouped", bufs=3))
-        w_pool = ctx.enter_context(tc.tile_pool(name="w_mx", bufs=3))
+        w_pool = ctx.enter_context(tc.tile_pool(name="w_mx", bufs=AHEAD + 2))
         rope_pool = ctx.enter_context(tc.tile_pool(name="rope", bufs=3))
-        result_pool = ctx.enter_context(tc.tile_pool(name="result", bufs=6))
+        result_pool = ctx.enter_context(tc.tile_pool(name="result", bufs=4))
         turned_pool = ctx.enter_context(tc.psum_pool(name="turned", bufs=4))
         product_pool = ctx.enter_context(tc.psum_pool(name="product", bufs=4))
         ctx.enter_context(tc.manual_schedule())
@@ -77,13 +78,10 @@ def tile_attention_pa_kernel(tc, x, freq_cos, freq_sin, wq, wk, out_0, out_1):
             scales = pool.tile([P, PASSES * SLAB], U8, name=label + "_scales", align_bytes=64)
             mx_tiles[n] = (codes, scales)
 
-        def quantise(n, half):
+        def quantise(n):
             codes, scales = mx_tiles[n]
-            cols = slice(half * 2 * SLAB, (half + 1) * 2 * SLAB)
             nc.vector.quantize_mx(
-                out=codes[:, cols].bitcast(FP8X4),
-                scales=scales[:, cols],
-                in_=grouped_tiles[n][:, half * 8 * SLAB : (half + 1) * 8 * SLAB],
+                out=codes[:].bitcast(FP8X4), scales=scales[:], in_=grouped_tiles[n][:]
             )
 
         def multiply(n, x_slab):
@@ -105,31 +103,27 @@ def tile_attention_pa_kernel(tc, x, freq_cos, freq_sin, wq, wk, out_0, out_1):
                     )
             return product
 
-        def rotate_and_store(product, x_slab, target):
+        def rope_products(product, from_even, from_odd):
             planes = product[:].rearrange("p (b i c) -> p b i c", b=2, i=2)
             twice = [P, 2, P, 2]
-            from_even = rope_pool.tile([P, BANK], F32)
             nc.vector.tensor_tensor(
-                out=from_even[:].rearrange("p (b c i) -> p b c i", b=2, i=2),
+                out=from_even.rearrange("p (b c i) -> p b c i", b=2, i=2),
                 in0=planes[:, :, 0, :].unsqueeze(3).to_broadcast(twice),
                 in1=cos_sin[:].rearrange("p (b c i) -> p b c i", b=2, i=2),
                 op=MULT,
             )
-            from_odd = rope_pool.tile([P, BANK], F32)
             nc.vector.tensor_tensor(
-                out=from_odd[:].rearrange("p (b c i) -> p b c i", b=2, i=2),
+                out=from_odd.rearrange("p (b c i) -> p b c i", b=2, i=2),
                 in0=planes[:, :, 1, :].unsqueeze(3).to_broadcast(twice),
                 in1=minus_sin_cos[:].rearrange("p (b c i) -> p b c i", b=2, i=2),
                 op=MULT,
             )
-            rotated = result_pool.tile([P, BANK], F32)
-            nc.gpsimd.tensor_tensor(out=rotated[:], in0=from_even[:], in1=from_odd[:], op=ADD)
+
+        def store(rotated, target):
             out, first_head = target
-            for entry in range(2):
+            for entry in range(B):
                 nc.sync.dma_start(
-                    out=out[2 * x_slab + entry, first_head : first_head + SLAB_HEADS].rearrange(
-                        "h s d -> s h d"
-                    ),
+                    out=out[entry, first_head : first_head + SLAB_HEADS].rearrange("h s d -> s h d"),
                     in_=rotated[:, entry * SLAB : (entry + 1) * SLAB].rearrange(
                         "p (h d) -> p h d", h=SLAB_HEADS
                     ),
@@ -157,21 +151,27 @@ def tile_attention_pa_kernel(tc, x, freq_cos, freq_sin, wq, wk, out_0, out_1):
         nc.vector.tensor_scalar_mul(out=minus_sin_cos_view[:, :, :, 0], in0=sin_repeated, scalar1=-1.0)
         nc.vector.tensor_copy(out=minus_sin_cos_view[:, :, :, 1], in_=cos_repeated)
 
-        for n in range(X_SLABS + 1):
+        for n in range(X_SLABS + AHEAD):
             transpose_and_regroup(n)
             new_mx_tiles(n)
-            quantise(n, 0)
-            quantise(n, 1)
+            quantise(n)
 
         last = len(slabs) - 1
         for n in range(X_SLABS, len(slabs)):
             if n - X_SLABS + RAW_BUFS <= last:
                 load(n - X_SLABS + RAW_BUFS)
-            if n < last:
-                transpose_and_regroup(n + 1)
-                new_mx_tiles(n + 1)
+            if n + AHEAD <= last:
+                transpose_and_regroup(n + AHEAD)
+                new_mx_tiles(n + AHEAD)
             products = [multiply(n, x_slab) for x_slab in range(X_SLABS)]
-            for part in range(2):
-                if n < last:
-                    quantise(n + 1, part)
-                rotate_and_store(products[part], part, targets[n - X_SLABS])
+            from_even = rope_pool.tile([P, X_SLABS * BANK], F32)
+            from_odd = rope_pool.tile([P, X_SLABS * BANK], F32)
+            for x_slab in range(X_SLABS):
+                bank_cols = slice(x_slab * BANK, (x_slab + 1) * BANK)
+                rope_products(products[x_slab], from_even[:, bank_cols], from_odd[:, bank_cols])
+            if n + AHEAD <= last:
+                quantise(n + AHEAD)
+            adder = nc.vector if n == last else nc.gpsimd
+            rotated = result_pool.tile([P, X_SLABS * BANK], F32)
+            adder.tensor_tensor(out=rotated[:], in0=from_even[:], in1=from_odd[:], op=ADD)
+            store(rotated, targets[n - X_SLABS])

@@ -103,19 +103,12 @@ def tile_attention_pa_kernel(tc, x, freq_cos, freq_sin, wq, wk, out_0, out_1):
                     )
             return product
 
-        def rope_products(product, from_even, from_odd):
-            planes = product[:].rearrange("p (b i c) -> p b i c", b=2, i=2)
-            twice = [P, 2, P, 2]
+        def rope_terms(product, terms):
+            shape = [P, 2, SLAB, 2]
             nc.vector.tensor_tensor(
-                out=from_even.rearrange("p (b c i) -> p b c i", b=2, i=2),
-                in0=planes[:, :, 0, :].unsqueeze(3).to_broadcast(twice),
-                in1=cos_sin[:].rearrange("p (b c i) -> p b c i", b=2, i=2),
-                op=MULT,
-            )
-            nc.vector.tensor_tensor(
-                out=from_odd.rearrange("p (b c i) -> p b c i", b=2, i=2),
-                in0=planes[:, :, 1, :].unsqueeze(3).to_broadcast(twice),
-                in1=minus_sin_cos[:].rearrange("p (b c i) -> p b c i", b=2, i=2),
+                out=terms.rearrange("p (b q i) -> p b q i", b=2, i=2),
+                in0=product[:].rearrange("p (b q) -> p b q", b=2).unsqueeze(3).to_broadcast(shape),
+                in1=factors[:].rearrange("p (q i) -> p q i", i=2).unsqueeze(1).to_broadcast(shape),
                 op=MULT,
             )
 
@@ -139,17 +132,14 @@ def tile_attention_pa_kernel(tc, x, freq_cos, freq_sin, wq, wk, out_0, out_1):
         ident = keep.tile([P, P], F32)
         make_identity(nc, ident[:])
 
-        repeats = BANK // HD
-        cos_sin = keep.tile([P, BANK], F32)
-        minus_sin_cos = keep.tile([P, BANK], F32)
-        cos_sin_view = cos_sin[:].rearrange("p (n j i) -> p n j i", n=repeats, i=2)
-        minus_sin_cos_view = minus_sin_cos[:].rearrange("p (n j i) -> p n j i", n=repeats, i=2)
-        cos_repeated = cos_bf[:].unsqueeze(1).to_broadcast([P, repeats, HALF])
-        sin_repeated = sin_bf[:].unsqueeze(1).to_broadcast([P, repeats, HALF])
-        nc.vector.tensor_copy(out=cos_sin_view[:, :, :, 0], in_=cos_repeated)
-        nc.vector.tensor_copy(out=cos_sin_view[:, :, :, 1], in_=sin_repeated)
-        nc.vector.tensor_scalar_mul(out=minus_sin_cos_view[:, :, :, 0], in0=sin_repeated, scalar1=-1.0)
-        nc.vector.tensor_copy(out=minus_sin_cos_view[:, :, :, 1], in_=cos_repeated)
+        factors = keep.tile([P, 2 * SLAB], F32)
+        factors_view = factors[:].rearrange("p (t h j i) -> p t h j i", t=2, h=SLAB_HEADS, i=2)
+        cos_repeated = cos_bf[:].unsqueeze(1).to_broadcast([P, SLAB_HEADS, HALF])
+        sin_repeated = sin_bf[:].unsqueeze(1).to_broadcast([P, SLAB_HEADS, HALF])
+        nc.vector.tensor_copy(out=factors_view[:, 0, :, :, 0], in_=cos_repeated)
+        nc.vector.tensor_copy(out=factors_view[:, 0, :, :, 1], in_=sin_repeated)
+        nc.vector.tensor_scalar_mul(out=factors_view[:, 1, :, :, 0], in0=sin_repeated, scalar1=-1.0)
+        nc.vector.tensor_copy(out=factors_view[:, 1, :, :, 1], in_=cos_repeated)
 
         for n in range(X_SLABS + AHEAD):
             transpose_and_regroup(n)
@@ -164,14 +154,18 @@ def tile_attention_pa_kernel(tc, x, freq_cos, freq_sin, wq, wk, out_0, out_1):
                 transpose_and_regroup(n + AHEAD)
                 new_mx_tiles(n + AHEAD)
             products = [multiply(n, x_slab) for x_slab in range(X_SLABS)]
-            from_even = rope_pool.tile([P, X_SLABS * BANK], F32)
-            from_odd = rope_pool.tile([P, X_SLABS * BANK], F32)
+            terms = rope_pool.tile([P, X_SLABS * 2 * BANK], F32)
             for x_slab in range(X_SLABS):
-                bank_cols = slice(x_slab * BANK, (x_slab + 1) * BANK)
-                rope_products(products[x_slab], from_even[:, bank_cols], from_odd[:, bank_cols])
+                rope_terms(products[x_slab], terms[:, x_slab * 2 * BANK : (x_slab + 1) * 2 * BANK])
             if n + AHEAD <= last:
                 quantise(n + AHEAD)
             adder = nc.vector if n == last else nc.gpsimd
-            rotated = result_pool.tile([P, X_SLABS * BANK], F32)
-            adder.tensor_tensor(out=rotated[:], in0=from_even[:], in1=from_odd[:], op=ADD)
+            rotated = result_pool.tile([P, B * SLAB], F32)
+            by_parity = terms[:].rearrange("p (b t f) -> p b t f", b=B, t=2)
+            adder.tensor_tensor(
+                out=rotated[:].rearrange("p (b f) -> p b f", b=B),
+                in0=by_parity[:, :, 0, :],
+                in1=by_parity[:, :, 1, :],
+                op=ADD,
+            )
             store(rotated, targets[n - X_SLABS])

from contextlib import ExitStack

import concourse.mybir as mybir
from concourse.masks import make_identity

F32 = mybir.dt.float32
BF16 = mybir.dt.bfloat16
U32 = mybir.dt.uint32
U8 = mybir.dt.uint8
FP8X4 = mybir.dt.float8_e4m3fn_x4
MULT = mybir.AluOpType.mult
ADD = mybir.AluOpType.add

B, S, D, H, HD = 4, 128, 2048, 16, 128
HALF = HD // 2
P = 128
K_PASS = 4 * P
PASSES = D // K_PASS
WORDS = D // 2
SLAB = 2 * P
SLAB_HEADS = SLAB // HD
X_SLABS = B * S // SLAB
W_SLABS = H * HD // SLAB
BANK = 512
RAW_BUFS = 12
AHEAD = 2

FLOPS = 2 * (B * S) * D * (2 * H * HD)


def tile_attention_pa_kernel(tc, x, freq_cos, freq_sin, wq, wk, out_0, out_1):
    nc = tc.nc

    slabs = [x[2 * n : 2 * n + 2].rearrange("b s k -> s b k") for n in range(X_SLABS)]
    for w in (wq, wk):
        for n in range(W_SLABS):
            slabs.append(w[n * SLAB : (n + 1) * SLAB, :].rearrange("(c i) k -> c i k", i=2))
    targets = [(out, n * SLAB_HEADS) for out in (out_0, out_1) for n in range(W_SLABS)]

    with ExitStack() as ctx:
        keep = ctx.enter_context(tc.tile_pool(name="keep", bufs=1))
        raw_pool = ctx.enter_context(tc.tile_pool(name="raw", bufs=RAW_BUFS))
        grouped_pool = ctx.enter_context(tc.tile_pool(name="grouped", bufs=3))
        w_pool = ctx.enter_context(tc.tile_pool(name="w_mx", bufs=AHEAD + 2))
        rope_pool = ctx.enter_context(tc.tile_pool(name="rope", bufs=3))
        result_pool = ctx.enter_context(tc.tile_pool(name="result", bufs=4))
        turned_pool = ctx.enter_context(tc.psum_pool(name="turned", bufs=4))
        product_pool = ctx.enter_context(tc.psum_pool(name="product", bufs=4))
        ctx.enter_context(tc.manual_schedule())

        raw_tiles = {}
        grouped_tiles = {}
        mx_tiles = {}

        def load(n):
            raw = raw_pool.tile([P, 2 * D], BF16)
            nc.sync.dma_start(out=raw[:].rearrange("p (r k) -> p r k", r=2), in_=slabs[n])
            raw_tiles[n] = raw

        def transpose_and_regroup(n):
            words = raw_tiles[n][:].bitcast(F32)
            grouped = grouped_pool.tile([P, PASSES * SLAB * 4], BF16, align_bytes=64)
            grouped_words = grouped[:].bitcast(F32).rearrange(
                "p (g r c u) -> p g r c u", g=PASSES, r=2, u=2
            )
            for g in range(PASSES):
                turned = turned_pool.tile([P, 2, 2, P], F32)
                for r in range(2):
                    for u in range(2):
                        first = r * WORDS + (2 * g + u) * P
                        nc.tensor.transpose(turned[:, r, u, :], words[:, first : first + P], ident[:])
                nc.scalar.copy(out=grouped_words[:, g], in_=turned[:].rearrange("p r u c -> p r c u"))
            grouped_tiles[n] = grouped

        def new_mx_tiles(n):
            pool, label = (keep, "x%d" % n) if n < X_SLABS else (w_pool, "w")
            codes = pool.tile([P, PASSES * SLAB], U32, name=label + "_codes", align_bytes=64)
            scales = pool.tile([P, PASSES * SLAB], U8, name=label + "_scales", align_bytes=64)
            mx_tiles[n] = (codes, scales)

        def quantise(n):
            codes, scales = mx_tiles[n]
            nc.vector.quantize_mx(
                out=codes[:].bitcast(FP8X4), scales=scales[:], in_=grouped_tiles[n][:]
            )

        def multiply(n, x_slab):
            x_codes, x_scales = mx_tiles[x_slab]
            w_codes, w_scales = mx_tiles[n]
            product = product_pool.tile([P, BANK], F32)
            for entry in range(2):
                for g in range(PASSES):
                    x_cols = slice(g * SLAB + entry * P, g * SLAB + (entry + 1) * P)
                    w_cols = slice(g * SLAB, (g + 1) * SLAB)
                    nc.tensor.matmul_mx(
                        out=product[:, entry * SLAB : (entry + 1) * SLAB],
                        lhsT=x_codes[:, x_cols].bitcast(FP8X4),
                        lhsT_scale=x_scales[:, x_cols],
                        rhs=w_codes[:, w_cols].bitcast(FP8X4),
                        rhs_scale=w_scales[:, w_cols],
                        start=(g == 0),
                        stop=(g == PASSES - 1),
                    )
            return product

        def rope_terms(product, terms):
            shape = [P, 2, SLAB, 2]
            nc.vector.tensor_tensor(
                out=terms.rearrange("p (b q i) -> p b q i", b=2, i=2),
                in0=product[:].rearrange("p (b q) -> p b q", b=2).unsqueeze(3).to_broadcast(shape),
                in1=factors[:].rearrange("p (q i) -> p q i", i=2).unsqueeze(1).to_broadcast(shape),
                op=MULT,
            )

        def store(rotated, target):
            out, first_head = target
            for entry in range(B):
                nc.sync.dma_start(
                    out=out[entry, first_head : first_head + SLAB_HEADS].rearrange("h s d -> s h d"),
                    in_=rotated[:, entry * SLAB : (entry + 1) * SLAB].rearrange(
                        "p (h d) -> p h d", h=SLAB_HEADS
                    ),
                )

        cos_bf = keep.tile([P, HALF], BF16)
        sin_bf = keep.tile([P, HALF], BF16)
        nc.scalar.dma_start(out=cos_bf[:], in_=freq_cos)
        nc.scalar.dma_start(out=sin_bf[:], in_=freq_sin)
        for n in range(RAW_BUFS):
            load(n)

        ident = keep.tile([P, P], F32)
        make_identity(nc, ident[:])

        factors = keep.tile([P, 2 * SLAB], F32)
        factors_view = factors[:].rearrange("p (t h j i) -> p t h j i", t=2, h=SLAB_HEADS, i=2)
        cos_repeated = cos_bf[:].unsqueeze(1).to_broadcast([P, SLAB_HEADS, HALF])
        sin_repeated = sin_bf[:].unsqueeze(1).to_broadcast([P, SLAB_HEADS, HALF])
        nc.vector.tensor_copy(out=factors_view[:, 0, :, :, 0], in_=cos_repeated)
        nc.vector.tensor_copy(out=factors_view[:, 0, :, :, 1], in_=sin_repeated)
        nc.vector.tensor_scalar_mul(out=factors_view[:, 1, :, :, 0], in0=sin_repeated, scalar1=-1.0)
        nc.vector.tensor_copy(out=factors_view[:, 1, :, :, 1], in_=cos_repeated)

        for n in range(X_SLABS + AHEAD):
            transpose_and_regroup(n)
            new_mx_tiles(n)
            quantise(n)

        last = len(slabs) - 1
        for n in range(X_SLABS, len(slabs)):
            if n - X_SLABS + RAW_BUFS <= last:
                load(n - X_SLABS + RAW_BUFS)
            if n + AHEAD <= last:
                transpose_and_regroup(n + AHEAD)
                new_mx_tiles(n + AHEAD)
            products = [multiply(n, x_slab) for x_slab in range(X_SLABS)]
            terms = rope_pool.tile([P, X_SLABS * 2 * BANK], F32)
            for x_slab in range(X_SLABS):
                rope_terms(products[x_slab], terms[:, x_slab * 2 * BANK : (x_slab + 1) * 2 * BANK])
            if n + AHEAD <= last:
                quantise(n + AHEAD)
            adder = nc.vector if n == last else nc.gpsimd
            rotated = result_pool.tile([P, B * SLAB], F32)
            by_parity = terms[:].rearrange("p (b t f) -> p b t f", b=B, t=2)
            adder.tensor_tensor(
                out=rotated[:].rearrange("p (b f) -> p b f", b=B),
                in0=by_parity[:, :, 0, :],
                in1=by_parity[:, :, 1, :],
                op=ADD,
            )
            store(rotated, targets[n - X_SLABS])
